import numpy as np
import ml_dtypes


def mxq(x, axis, fmt="e4m3"):
    dtype, down = {"e4m3": (ml_dtypes.float8_e4m3fn, 7), "e5m2": (ml_dtypes.float8_e5m2, 14)}[fmt]
    v = np.moveaxis(np.asarray(x, np.float32).astype(ml_dtypes.bfloat16).astype(np.float64), axis, -1)
    blocks = v.reshape(v.shape[:-1] + (-1, 32))
    amax = np.abs(blocks).max(-1, keepdims=True)
    byte = np.maximum(np.where(amax > 0, np.frexp(amax)[1] - 1 + 127, 0) - down, 1)
    scale = np.exp2(byte - 127.0)
    codes = (blocks / scale).astype(np.float32).astype(dtype).astype(np.float64)
    return np.moveaxis((codes * scale).reshape(v.shape), -1, axis)


WIDE = False


def mx_kscale(k):
    if not WIDE:
        return np.ones(k)
    levels = np.array([10, -10, 5, -5, 0])
    if k % 512:
        return np.exp2(np.random.permutation(np.resize(levels, k // 32))).repeat(32)
    a = np.empty((k // 512, 16))
    for p in range(k // 512):
        a[p, :8] = np.random.permutation(np.resize(levels, 8))
        for g in range(8):
            far = levels[np.abs(levels - a[p, g]) >= 10]
            a[p, g + 8] = far[np.random.randint(len(far))]
    return np.exp2(a.ravel()).repeat(32)


BF16 = ml_dtypes.bfloat16


def bf(x):
    return np.asarray(x, np.float32).astype(BF16)


def f64(x):
    return np.asarray(x).astype(np.float64)


N, C = 4096, 512
KS = 3 * C
SQRT3 = np.sqrt(3.0)
EPS = 1e-6


def setup_inputs():
    t = mx_kscale(KS)
    return {"s": bf(np.random.standard_normal((N, C))),
            "v": bf(np.random.standard_normal((N, C, 3))),
            "g_s": bf(np.random.standard_normal((N, KS)) * t),
            "w0": bf(np.random.standard_normal((KS, C)) / t[:, None]),
            "ln_g0": bf(1.0 + 0.1 * np.random.standard_normal(C))}


def reference(s, v, g_s, w0, ln_g0):
    s, v = f64(s), f64(v)
    ss = s * s
    vv0 = np.sum(v * v, axis=-1) / SQRT3
    sc = np.concatenate([s, ss, vv0], axis=-1) * f64(g_s)
    y = s + (mxq(sc, 1, "e4m3") @ mxq(f64(w0), 0, "e4m3")) / np.sqrt(KS)
    mu = np.mean(y, axis=-1, keepdims=True)
    sd = np.sqrt(np.mean((y - mu) ** 2, axis=-1, keepdims=True) + EPS)
    return (y - mu) / sd * f64(ln_g0)

@@ -1,0 +1,308 @@
+import math
+
+import concourse.mybir as mybir
+from concourse.masks import make_identity
+
+F32 = mybir.dt.float32
+BF16 = mybir.dt.bfloat16
+U32 = mybir.dt.uint32
+U8 = mybir.dt.uint8
+FP8X4 = mybir.dt.float8_e4m3fn_x4
+MULT = mybir.AluOpType.mult
+ADD = mybir.AluOpType.add
+SQUARE = mybir.ActivationFunctionType.Square
+SQRT = mybir.ActivationFunctionType.Sqrt
+
+P = 128
+POINTS = 4096
+C = 512
+XYZ = 3
+PASSES = 3
+KS = PASSES * C
+PACK = 4
+HALVES = 2
+PAIR = 2
+WORDS = C // PAIR
+R = 2
+CHUNKS = POINTS // (P * R)
+EPS = 1e-6
+
+FLOPS = 2 * POINTS * KS * C
+
+
+def tile_selfinteraction_pc_t_kernel(tc, s, v, g_s, w0, ln_g0, out):
+    nc = tc.nc
+
+    s_chunks = s.rearrange("(k p r) c -> k p (r c)", p=P, r=R)
+    g_chunks = g_s.rearrange("(k p r) c -> k p (r c)", p=P, r=R)
+    v_chunks = v.rearrange("(k p r) c j -> k p (r c j)", p=P, r=R)
+    out_chunks = out.rearrange("(k p r) c -> k p (r c)", p=P, r=R)
+
+    with tc.tile_pool(name="keep", bufs=1) as keep, tc.tile_pool(name="loads", bufs=3) as loads, tc.tile_pool(
+        name="work", bufs=2
+    ) as work, tc.tile_pool(name="small", bufs=3) as small, tc.psum_pool(
+        name="psum", bufs=2
+    ) as psum, tc.manual_schedule():
+        held = {}
+
+        ident = keep.tile([P, P], F32)
+        make_identity(nc, ident[:])
+        eps = keep.tile([P, 1], F32)
+        nc.vector.memset(eps[:], EPS)
+        w_rows = keep.tile([P, PASSES * PACK * C], BF16)
+        gain = keep.tile([P, C], BF16)
+        w_codes = keep.tile([P, PASSES * C], U32, align_bytes=64)
+        w_scales = keep.tile([P, PASSES * C], U8, align_bytes=64)
+
+        def load_weights():
+            nc.sync.dma_start(
+                out=w_rows[:].rearrange("p (g x) -> p g x", g=PASSES),
+                in_=w0.rearrange("(g p t) c -> p g (t c)", g=PASSES, p=P, t=PACK),
+            )
+            nc.sync.dma_start(out=gain[:], in_=ln_g0.partition_broadcast(P))
+
+        def quantise_weights():
+            grouped = []
+            for g in range(PASSES):
+                w_grouped = keep.tile([P, C * PACK], BF16, align_bytes=64, bufs=PASSES)
+                nc.vector.tensor_copy(
+                    out=w_grouped[:].rearrange("p (c t) -> p c t", t=PACK),
+                    in_=w_rows[:, g * PACK * C : (g + 1) * PACK * C].rearrange("p (t c) -> p c t", t=PACK),
+                )
+                grouped.append(w_grouped)
+            for g in range(PASSES):
+                nc.vector.quantize_mx(
+                    out=w_codes[:, g * C : (g + 1) * C].bitcast(FP8X4),
+                    scales=w_scales[:, g * C : (g + 1) * C],
+                    in_=grouped[g][:],
+                )
+
+        def load(c):
+            s_t = loads.tile([P, R * C], BF16, bufs=5)
+            nc.sync.dma_start(out=s_t[:], in_=s_chunks[c])
+            v_t = loads.tile([P, R * C * XYZ], BF16)
+            nc.sync.dma_start(out=v_t[:], in_=v_chunks[c])
+            g_t = loads.tile([P, R * KS], BF16)
+            nc.sync.dma_start(out=g_t[:], in_=g_chunks[c])
+            held["s", c], held["v", c], held["g", c] = s_t, v_t, g_t
+
+        def square_s(c):
+            ss = work.tile([P, R * C], F32)
+            nc.scalar.activation(out=ss[:], in_=held["s", c][:], func=SQUARE)
+            held["ss", c] = ss
+
+        def gate_products(c):
+            g_rows = held["g", c][:].rearrange("p (r g c) -> p r g c", r=R, g=PASSES)
+            u01 = work.tile([P, R * 2 * C], BF16)
+            u01_rows = u01[:].rearrange("p (r g c) -> p r g c", r=R, g=2)
+            nc.vector.tensor_tensor(
+                out=u01_rows[:, :, 0, :],
+                in0=held["s", c][:].rearrange("p (r c) -> p r c", r=R),
+                in1=g_rows[:, :, 0, :],
+                op=MULT,
+            )
+            nc.vector.tensor_tensor(
+                out=u01_rows[:, :, 1, :],
+                in0=held["ss", c][:].rearrange("p (r c) -> p r c", r=R),
+                in1=g_rows[:, :, 1, :],
+                op=MULT,
+            )
+            held["u01", c] = u01
+
+        def square_v(c):
+            for r in range(R):
+                v_sq = work.tile([P, C * XYZ], F32)
+                nc.scalar.activation(out=v_sq[:], in_=held["v", c][:, r * C * XYZ : (r + 1) * C * XYZ], func=SQUARE)
+                held["v_sq", c, r] = v_sq
+
+        def transpose_words(c):
+            g_words = held["g", c][:].bitcast(F32)
+            u01_words = held["u01", c][:].bitcast(F32)
+            gate_bank = psum.tile([P, R * WORDS], F32)
+            for r in range(R):
+                for h in range(HALVES):
+                    first = (r * PASSES + 2) * WORDS
+                    nc.tensor.transpose(
+                        gate_bank[:, (r * HALVES + h) * P : (r * HALVES + h + 1) * P],
+                        g_words[:, first + h : first + WORDS : HALVES],
+                        ident[:],
+                    )
+            banks = []
+            for r in range(R):
+                u01_bank = psum.tile([P, 2 * WORDS], F32)
+                for b in range(2 * HALVES):
+                    g, h = divmod(b, HALVES)
+                    first = (r * 2 + g) * WORDS
+                    nc.tensor.transpose(
+                        u01_bank[:, b * P : (b + 1) * P], u01_words[:, first + h : first + WORDS : HALVES], ident[:]
+                    )
+                banks.append(u01_bank)
+            gate_t = work.tile([P, R * WORDS], F32)
+            nc.scalar.copy(
+                out=gate_t[:].rearrange("p (r n h) -> p r n h", r=R, h=HALVES),
+                in_=gate_bank[:].rearrange("p (r h n) -> p r n h", r=R, h=HALVES),
+            )
+            u01_grouped = work.tile([P, R * 2 * WORDS], F32, align_bytes=64)
+            for r in range(R):
+                nc.scalar.copy(
+                    out=u01_grouped[:, r * 2 * WORDS : (r + 1) * 2 * WORDS].rearrange(
+                        "p (g n h) -> p g n h", g=2, h=HALVES
+                    ),
+                    in_=banks[r][:].rearrange("p (g h n) -> p g n h", g=2, h=HALVES),
+                )
+            held["gate_t", c], held["u01_grouped", c] = gate_t, u01_grouped
+
+        def sum_squares(c):
+            for r in range(R):
+                planes = held["v_sq", c, r][:].rearrange("n (q h e j) -> n h e j q", h=HALVES, q=P, e=PAIR, j=XYZ)
+                vv_bank = psum.tile([P, PACK * P], F32)
+                for h in range(HALVES):
+                    for e in range(PAIR):
+                        t = PAIR * h + e
+                        for j in range(XYZ):
+                            nc.tensor.matmul(
+                                vv_bank[:, t * P : (t + 1) * P],
+                                lhsT=planes[:, h, e, j, :],
+                                rhs=ident[:],
+                                is_transpose=True,
+                                start=(j == 0),
+                                stop=(j == XYZ - 1),
+                            )
+                held["vv", c, r] = vv_bank
+
+        def quantise_01(c):
+            codes01 = work.tile([P, R * 2 * P], U32, align_bytes=64)
+            scales01 = work.tile([P, R * 2 * P], U8, align_bytes=64)
+            nc.vector.quantize_mx(
+                out=codes01[:].bitcast(FP8X4), scales=scales01[:], in_=held["u01_grouped", c][:].bitcast(BF16)
+            )
+            held["codes01", c], held["scales01", c] = codes01, scales01
+
+        def gate_vv(c):
+            gate_values = held["gate_t", c][:].bitcast(BF16)
+            u2_grouped = work.tile([P, R * C], BF16, align_bytes=64)
+            for r in range(R):
+                nc.vector.scalar_tensor_tensor(
+                    out=u2_grouped[:, r * C : (r + 1) * C].rearrange("p (n t) -> p n t", t=PACK),
+                    in0=held["vv", c, r][:].rearrange("p (t n) -> p n t", t=PACK),
+                    scalar=1.0 / math.sqrt(3.0),
+                    in1=gate_values[:, r * C : (r + 1) * C].rearrange("p (n t) -> p n t", t=PACK),
+                    op0=MULT,
+                    op1=MULT,
+                )
+            held["u2_grouped", c] = u2_grouped
+
+        def quantise_2(c):
+            codes2 = work.tile([P, R * P], U32, align_bytes=64)
+            scales2 = work.tile([P, R * P], U8, align_bytes=64)
+            nc.vector.quantize_mx(out=codes2[:].bitcast(FP8X4), scales=scales2[:], in_=held["u2_grouped", c][:])
+            held["codes2", c], held["scales2", c] = codes2, scales2
+
+        def multiply(c):
+            for r in range(R):
+                acc = psum.tile([P, C], F32)
+                for g in range(PASSES):
+                    if g < 2:
+                        codes, scales, first = held["codes01", c], held["scales01", c], (r * 2 + g) * P
+                    else:
+                        codes, scales, first = held["codes2", c], held["scales2", c], r * P
+                    nc.tensor.matmul_mx(
+                        out=acc[:],
+                        lhsT=codes[:, first : first + P].bitcast(FP8X4),
+                        lhsT_scale=scales[:, first : first + P],
+                        rhs=w_codes[:, g * C : (g + 1) * C].bitcast(FP8X4),
+                        rhs_scale=w_scales[:, g * C : (g + 1) * C],
+                        start=(g == 0),
+                        stop=(g == PASSES - 1),
+                    )
+                held["acc", c, r] = acc
+
+        def residual(c):
+            y = work.tile([P, R * C], F32)
+            y_sum = small.tile([P, R], F32)
+            for r in range(R):
+                nc.vector.scalar_tensor_tensor(
+                    out=y[:, r * C : (r + 1) * C],
+                    in0=held["acc", c, r][:],
+                    scalar=1.0 / math.sqrt(KS),
+                    in1=held["s", c][:, r * C : (r + 1) * C],
+                    op0=MULT,
+                    op1=ADD,
+                    accum_out=y_sum[:, r : r + 1],
+                )
+            neg_mean = small.tile([P, R], F32)
+            nc.vector.tensor_scalar(out=neg_mean[:], in0=y_sum[:], scalar1=-1.0 / C, scalar2=None, op0=MULT)
+            held["y", c], held["neg_mean", c] = y, neg_mean
+
+        def centre(c):
+            y, neg_mean = held["y", c], held["neg_mean", c]
+            sq_sum = small.tile([P, R], F32)
+            centred = work.tile([P, R * C], F32)
+            for r in range(R):
+                cols = slice(r * C, (r + 1) * C)
+                squares = work.tile([P, C], BF16)
+                nc.scalar.activation(
+                    out=squares[:],
+                    in_=y[:, cols],
+                    func=SQUARE,
+                    bias=neg_mean[:, r : r + 1],
+                    accum_out=sq_sum[:, r : r + 1],
+                )
+                nc.vector.scalar_tensor_tensor(
+                    out=centred[:, cols],
+                    in0=y[:, cols],
+                    scalar=neg_mean[:, r : r + 1],
+                    in1=gain[:],
+                    op0=ADD,
+                    op1=MULT,
+                )
+            held["sq_sum", c], held["centred", c] = sq_sum, centred
+
+        def deviation(c):
+            sd = small.tile([P, R], F32)
+            nc.scalar.activation(out=sd[:], in_=held["sq_sum", c][:], func=SQRT, bias=eps[:, 0:1], scale=1.0 / C)
+            inv_sd = small.tile([P, R], F32)
+            nc.vector.reciprocal(out=inv_sd[:], in_=sd[:])
+            held["inv_sd", c] = inv_sd
+
+        def scale_and_store(c):
+            result = work.tile([P, R * C], F32, bufs=3)
+            for r in range(R):
+                cols = slice(r * C, (r + 1) * C)
+                nc.vector.tensor_scalar(
+                    out=result[:, cols],
+                    in0=held["centred", c][:, cols],
+                    scalar1=held["inv_sd", c][:, r : r + 1],
+                    scalar2=None,
+                    op0=MULT,
+                )
+            nc.sync.dma_start(out=out_chunks[c], in_=result[:])
+
+        def run(stage, c):
+            if 0 <= c < CHUNKS:
+                stage(c)
+
+        def step(i):
+            run(transpose_words, i)
+            run(sum_squares, i)
+            run(gate_products, i + 1)
+            run(centre, i - 2)
+            run(quantise_01, i)
+            run(gate_vv, i)
+            run(deviation, i - 2)
+            run(scale_and_store, i - 2)
+            run(quantise_2, i)
+            run(square_v, i + 1)
+            run(multiply, i - 1)
+            run(residual, i - 1)
+            run(square_s, i + 2)
+            run(load, i + 3)
+
+        step(-3)
+        step(-2)
+        load_weights()
+        step(-1)
+        step(0)
+        quantise_weights()
+        for i in range(1, CHUNKS + 2):
+            step(i)

@@ -21,10 +21,11 @@ PASSES = 3
 KS = PASSES * C
 PACK = 4
 HALVES = 2
-PAIR = 2
-WORDS = C // PAIR
+WORDS = C // 2
 R = 2
 CHUNKS = POINTS // (P * R)
+TILES = CHUNKS * R
+AHEAD = 4
 EPS = 1e-6
 
 FLOPS = 2 * POINTS * KS * C
@@ -38,9 +39,9 @@ def tile_selfinteraction_pc_t_kernel(tc, s, v, g_s, w0, ln_g0, out):
     v_chunks = v.rearrange("(k p r) c j -> k p (r c j)", p=P, r=R)
     out_chunks = out.rearrange("(k p r) c -> k p (r c)", p=P, r=R)
 
-    with tc.tile_pool(name="keep", bufs=1) as keep, tc.tile_pool(name="loads", bufs=3) as loads, tc.tile_pool(
-        name="work", bufs=2
-    ) as work, tc.tile_pool(name="small", bufs=3) as small, tc.psum_pool(
+    with tc.tile_pool(name="keep", bufs=1) as keep, tc.tile_pool(name="loads", bufs=AHEAD + 2) as loads, tc.tile_pool(
+        name="work", bufs=3
+    ) as work, tc.tile_pool(name="small", bufs=4) as small, tc.psum_pool(
         name="psum", bufs=2
     ) as psum, tc.manual_schedule():
         held = {}
@@ -50,6 +51,7 @@ def tile_selfinteraction_pc_t_kernel(tc, s, v, g_s, w0, ln_g0, out):
         eps = keep.tile([P, 1], F32)
         nc.vector.memset(eps[:], EPS)
         w_rows = keep.tile([P, PASSES * PACK * C], BF16)
+        w_grouped = keep.tile([P, PASSES * C * PACK], BF16, align_bytes=64)
         gain = keep.tile([P, C], BF16)
         w_codes = keep.tile([P, PASSES * C], U32, align_bytes=64)
         w_scales = keep.tile([P, PASSES * C], U8, align_bytes=64)
@@ -59,250 +61,266 @@ def tile_selfinteraction_pc_t_kernel(tc, s, v, g_s, w0, ln_g0, out):
                 out=w_rows[:].rearrange("p (g x) -> p g x", g=PASSES),
                 in_=w0.rearrange("(g p t) c -> p g (t c)", g=PASSES, p=P, t=PACK),
             )
+
+        def load_gain():
             nc.sync.dma_start(out=gain[:], in_=ln_g0.partition_broadcast(P))
 
         def quantise_weights():
-            grouped = []
-            for g in range(PASSES):
-                w_grouped = keep.tile([P, C * PACK], BF16, align_bytes=64, bufs=PASSES)
-                nc.vector.tensor_copy(
-                    out=w_grouped[:].rearrange("p (c t) -> p c t", t=PACK),
-                    in_=w_rows[:, g * PACK * C : (g + 1) * PACK * C].rearrange("p (t c) -> p c t", t=PACK),
-                )
-                grouped.append(w_grouped)
+            def grouped(g):
+                return w_grouped[:, g * C * PACK : (g + 1) * C * PACK].rearrange("p (c t) -> p c t", t=PACK)
+
+            def rows(g):
+                return w_rows[:, g * PACK * C : (g + 1) * PACK * C].rearrange("p (t c) -> p c t", t=PACK)
+
+            nc.gpsimd.tensor_scalar(out=grouped(2), in0=rows(2), scalar1=1.0, scalar2=0.0, op0=MULT, op1=ADD)
+            for g in range(2):
+                nc.vector.tensor_copy(out=grouped(g), in_=rows(g))
             for g in range(PASSES):
                 nc.vector.quantize_mx(
                     out=w_codes[:, g * C : (g + 1) * C].bitcast(FP8X4),
                     scales=w_scales[:, g * C : (g + 1) * C],
-                    in_=grouped[g][:],
+                    in_=w_grouped[:, g * C * PACK : (g + 1) * C * PACK],
                 )
 
         def load(c):
-            s_t = loads.tile([P, R * C], BF16, bufs=5)
-            nc.sync.dma_start(out=s_t[:], in_=s_chunks[c])
             v_t = loads.tile([P, R * C * XYZ], BF16)
-            nc.sync.dma_start(out=v_t[:], in_=v_chunks[c])
+            s_t = loads.tile([P, R * C], BF16)
             g_t = loads.tile([P, R * KS], BF16)
-            nc.sync.dma_start(out=g_t[:], in_=g_chunks[c])
+            parts = R if c == 0 else 1
+            for part in range(parts):
+                for held_tile, rows in ((v_t, v_chunks[c]), (s_t, s_chunks[c]), (g_t, g_chunks[c])):
+                    width = rows.shape[1] // parts
+                    cols = slice(part * width, (part + 1) * width)
+                    nc.sync.dma_start(out=held_tile[:, cols], in_=rows[:, cols])
             held["s", c], held["v", c], held["g", c] = s_t, v_t, g_t
 
-        def square_s(c):
-            ss = work.tile([P, R * C], F32)
-            nc.scalar.activation(out=ss[:], in_=held["s", c][:], func=SQUARE)
-            held["ss", c] = ss
+        def square_v(i):
+            c, r = divmod(i, R)
+            v_sq = work.tile([P, C * XYZ], F32)
+            nc.scalar.activation(out=v_sq[:], in_=held["v", c][:, r * C * XYZ : (r + 1) * C * XYZ], func=SQUARE)
+            held["v_sq", i] = v_sq
 
-        def gate_products(c):
-            g_rows = held["g", c][:].rearrange("p (r g c) -> p r g c", r=R, g=PASSES)
-            u01 = work.tile([P, R * 2 * C], BF16)
-            u01_rows = u01[:].rearrange("p (r g c) -> p r g c", r=R, g=2)
-            nc.vector.tensor_tensor(
-                out=u01_rows[:, :, 0, :],
-                in0=held["s", c][:].rearrange("p (r c) -> p r c", r=R),
-                in1=g_rows[:, :, 0, :],
-                op=MULT,
-            )
-            nc.vector.tensor_tensor(
-                out=u01_rows[:, :, 1, :],
-                in0=held["ss", c][:].rearrange("p (r c) -> p r c", r=R),
-                in1=g_rows[:, :, 1, :],
-                op=MULT,
-            )
-            held["u01", c] = u01
-
-        def square_v(c):
-            for r in range(R):
-                v_sq = work.tile([P, C * XYZ], F32)
-                nc.scalar.activation(out=v_sq[:], in_=held["v", c][:, r * C * XYZ : (r + 1) * C * XYZ], func=SQUARE)
-                held["v_sq", c, r] = v_sq
-
-        def transpose_words(c):
-            g_words = held["g", c][:].bitcast(F32)
-            u01_words = held["u01", c][:].bitcast(F32)
-            gate_bank = psum.tile([P, R * WORDS], F32)
-            for r in range(R):
+        def transpose_words(i):
+            c, r = divmod(i, R)
+            s_words = held["s", c][:, r * C : (r + 1) * C].bitcast(F32)
+            g_words = held["g", c][:, r * KS : (r + 1) * KS].bitcast(F32)
+            s_g2_bank = psum.tile([P, 2 * WORDS], F32)
+            g01_bank = psum.tile([P, 2 * WORDS], F32)
+            for bank, place, words, first in (
+                (s_g2_bank, 0, s_words, 0),
+                (s_g2_bank, 1, g_words, 2 * WORDS),
+                (g01_bank, 0, g_words, 0),
+                (g01_bank, 1, g_words, WORDS),
+            ):
                 for h in range(HALVES):
-                    first = (r * PASSES + 2) * WORDS
+                    b = place * HALVES + h
                     nc.tensor.transpose(
-                        gate_bank[:, (r * HALVES + h) * P : (r * HALVES + h + 1) * P],
-                        g_words[:, first + h : first + WORDS : HALVES],
-                        ident[:],
+                        bank[:, b * P : (b + 1) * P], words[:, first + h : first + WORDS : HALVES], ident[:]
                     )
-            banks = []
-            for r in range(R):
-                u01_bank = psum.tile([P, 2 * WORDS], F32)
-                for b in range(2 * HALVES):
-                    g, h = divmod(b, HALVES)
-                    first = (r * 2 + g) * WORDS
-                    nc.tensor.transpose(
-                        u01_bank[:, b * P : (b + 1) * P], u01_words[:, first + h : first + WORDS : HALVES], ident[:]
+            held["s_g2_bank", i], held["g01_bank", i] = s_g2_bank, g01_bank
+
+        def sum_squares(i):
+            planes = held["v_sq", i][:].rearrange("n (q t j) -> n t j q", t=PACK, j=XYZ)
+            vv_bank = psum.tile([P, PACK * P], F32)
+            for t in range(PACK):
+                for j in range(XYZ):
+                    nc.tensor.matmul(
+                        vv_bank[:, t * P : (t + 1) * P],
+                        lhsT=planes[:, t, j, :],
+                        rhs=ident[:],
+                        is_transpose=True,
+                        start=(j == 0),
+                        stop=(j == XYZ - 1),
                     )
-                banks.append(u01_bank)
-            gate_t = work.tile([P, R * WORDS], F32)
+            held["vv_bank", i] = vv_bank
+
+        def copy_s_g2(i):
+            s_g2 = work.tile([P, 2 * WORDS], F32)
             nc.scalar.copy(
-                out=gate_t[:].rearrange("p (r n h) -> p r n h", r=R, h=HALVES),
-                in_=gate_bank[:].rearrange("p (r h n) -> p r n h", r=R, h=HALVES),
+                out=s_g2[:].rearrange("p (x n h) -> p x n h", x=2, h=HALVES),
+                in_=held["s_g2_bank", i][:].rearrange("p (x h n) -> p x n h", x=2, h=HALVES),
             )
-            u01_grouped = work.tile([P, R * 2 * WORDS], F32, align_bytes=64)
-            for r in range(R):
-                nc.scalar.copy(
-                    out=u01_grouped[:, r * 2 * WORDS : (r + 1) * 2 * WORDS].rearrange(
-                        "p (g n h) -> p g n h", g=2, h=HALVES
-                    ),
-                    in_=banks[r][:].rearrange("p (g h n) -> p g n h", g=2, h=HALVES),
-                )
-            held["gate_t", c], held["u01_grouped", c] = gate_t, u01_grouped
+            held["s_t", i] = s_g2[:, :WORDS].bitcast(BF16)
+            held["g2_t", i] = s_g2[:, WORDS:].bitcast(BF16)
 
-        def sum_squares(c):
-            for r in range(R):
-                planes = held["v_sq", c, r][:].rearrange("n (q h e j) -> n h e j q", h=HALVES, q=P, e=PAIR, j=XYZ)
-                vv_bank = psum.tile([P, PACK * P], F32)
-                for h in range(HALVES):
-                    for e in range(PAIR):
-                        t = PAIR * h + e
-                        for j in range(XYZ):
-                            nc.tensor.matmul(
-                                vv_bank[:, t * P : (t + 1) * P],
-                                lhsT=planes[:, h, e, j, :],
-                                rhs=ident[:],
-                                is_transpose=True,
-                                start=(j == 0),
-                                stop=(j == XYZ - 1),
-                            )
-                held["vv", c, r] = vv_bank
+        def square_s(i):
+            ss_t = work.tile([P, C], F32)
+            nc.scalar.activation(out=ss_t[:], in_=held["s_t", i], func=SQUARE)
+            held["ss_t", i] = ss_t
 
-        def quantise_01(c):
-            codes01 = work.tile([P, R * 2 * P], U32, align_bytes=64)
-            scales01 = work.tile([P, R * 2 * P], U8, align_bytes=64)
+        def product(i, g, factor):
+            gate = held["g01_bank", i][:, g * WORDS : (g + 1) * WORDS].bitcast(BF16)
+            nc.vector.tensor_tensor(
+                out=held["u", i][:, g * C : (g + 1) * C].rearrange("p (n h e) -> p n h e", h=HALVES, e=2),
+                in0=gate.rearrange("p (h n e) -> p n h e", h=HALVES, e=2),
+                in1=factor.rearrange("p (n h e) -> p n h e", h=HALVES, e=2),
+                op=MULT,
+            )
+
+        def product_0(i):
+            u = work.tile([P, KS], BF16, align_bytes=64)
+            held["u", i] = u
+            product(i, 0, held["s_t", i])
+
+        def product_1(i):
+            product(i, 1, held["ss_t", i][:])
+
+        def product_2(i):
+            nc.vector.scalar_tensor_tensor(
+                out=held["u", i][:, 2 * C :].rearrange("p (n t) -> p n t", t=PACK),
+                in0=held["vv_bank", i][:].rearrange("p (t n) -> p n t", t=PACK),
+                scalar=1.0 / math.sqrt(3.0),
+                in1=held["g2_t", i].rearrange("p (n t) -> p n t", t=PACK),
+                op0=MULT,
+                op1=MULT,
+            )
+
+        def quantise_01(i):
+            codes = work.tile([P, PASSES * P], U32, align_bytes=64)
+            scales = work.tile([P, PASSES * P], U8, align_bytes=64)
+            held["codes", i], held["scales", i] = codes, scales
             nc.vector.quantize_mx(
-                out=codes01[:].bitcast(FP8X4), scales=scales01[:], in_=held["u01_grouped", c][:].bitcast(BF16)
+                out=codes[:, : 2 * P].bitcast(FP8X4), scales=scales[:, : 2 * P], in_=held["u", i][:, : 2 * C]
             )
-            held["codes01", c], held["scales01", c] = codes01, scales01
 
-        def gate_vv(c):
-            gate_values = held["gate_t", c][:].bitcast(BF16)
-            u2_grouped = work.tile([P, R * C], BF16, align_bytes=64)
-            for r in range(R):
-                nc.vector.scalar_tensor_tensor(
-                    out=u2_grouped[:, r * C : (r + 1) * C].rearrange("p (n t) -> p n t", t=PACK),
-                    in0=held["vv", c, r][:].rearrange("p (t n) -> p n t", t=PACK),
-                    scalar=1.0 / math.sqrt(3.0),
-                    in1=gate_values[:, r * C : (r + 1) * C].rearrange("p (n t) -> p n t", t=PACK),
-                    op0=MULT,
-                    op1=MULT,
+        def quantise_2(i):
+            nc.vector.quantize_mx(
+                out=held["codes", i][:, 2 * P :].bitcast(FP8X4),
+                scales=held["scales", i][:, 2 * P :],
+                in_=held["u", i][:, 2 * C :],
+            )
+
+        def multiply(i):
+            acc = psum.tile([P, C], F32)
+            for g in range(PASSES):
+                nc.tensor.matmul_mx(
+                    out=acc[:],
+                    lhsT=held["codes", i][:, g * P : (g + 1) * P].bitcast(FP8X4),
+                    lhsT_scale=held["scales", i][:, g * P : (g + 1) * P],
+                    rhs=w_codes[:, g * C : (g + 1) * C].bitcast(FP8X4),
+                    rhs_scale=w_scales[:, g * C : (g + 1) * C],
+                    start=(g == 0),
+                    stop=(g == PASSES - 1),
                 )
-            held["u2_grouped", c] = u2_grouped
+            held["acc", i] = acc
 
-        def quantise_2(c):
-            codes2 = work.tile([P, R * P], U32, align_bytes=64)
-            scales2 = work.tile([P, R * P], U8, align_bytes=64)
-            nc.vector.quantize_mx(out=codes2[:].bitcast(FP8X4), scales=scales2[:], in_=held["u2_grouped", c][:])
-            held["codes2", c], held["scales2", c] = codes2, scales2
+        def residual(i):
+            c, r = divmod(i, R)
+            if r == 0:
+                y = work.tile([P, R * C], F32, bufs=4)
+                y_sum = small.tile([P, R], F32)
+                held["y", c], held["y_sum", c] = y, y_sum
+            nc.vector.scalar_tensor_tensor(
+                out=held["y", c][:, r * C : (r + 1) * C],
+                in0=held["acc", i][:],
+                scalar=1.0 / math.sqrt(KS),
+                in1=held["s", c][:, r * C : (r + 1) * C],
+                op0=MULT,
+                op1=ADD,
+                accum_out=held["y_sum", c][:, r : r + 1],
+            )
 
-        def multiply(c):
-            for r in range(R):
-                acc = psum.tile([P, C], F32)
-                for g in range(PASSES):
-                    if g < 2:
-                        codes, scales, first = held["codes01", c], held["scales01", c], (r * 2 + g) * P
-                    else:
-                        codes, scales, first = held["codes2", c], held["scales2", c], r * P
-                    nc.tensor.matmul_mx(
-                        out=acc[:],
-                        lhsT=codes[:, first : first + P].bitcast(FP8X4),
-                        lhsT_scale=scales[:, first : first + P],
-                        rhs=w_codes[:, g * C : (g + 1) * C].bitcast(FP8X4),
-                        rhs_scale=w_scales[:, g * C : (g + 1) * C],
-                        start=(g == 0),
-                        stop=(g == PASSES - 1),
-                    )
-                held["acc", c, r] = acc
+        def sum_deviations(i):
+            c, r = divmod(i, R)
+            if r == 0:
+                sq_sum = small.tile([P, R], F32)
+                held["sq_sum", c] = sq_sum
+            squares = work.tile([P, C], BF16)
+            nc.scalar.activation(
+                out=squares[:],
+                in_=held["y", c][:, r * C : (r + 1) * C],
+                func=SQUARE,
+                bias=held["y_sum", c][:, r : r + 1],
+                scale=-float(C),
+                accum_out=held["sq_sum", c][:, r : r + 1],
+            )
 
-        def residual(c):
-            y = work.tile([P, R * C], F32)
-            y_sum = small.tile([P, R], F32)
-            for r in range(R):
-                nc.vector.scalar_tensor_tensor(
-                    out=y[:, r * C : (r + 1) * C],
-                    in0=held["acc", c, r][:],
-                    scalar=1.0 / math.sqrt(KS),
-                    in1=held["s", c][:, r * C : (r + 1) * C],
-                    op0=MULT,
-                    op1=ADD,
-                    accum_out=y_sum[:, r : r + 1],
-                )
+        def negate_mean(c):
             neg_mean = small.tile([P, R], F32)
-            nc.vector.tensor_scalar(out=neg_mean[:], in0=y_sum[:], scalar1=-1.0 / C, scalar2=None, op0=MULT)
-            held["y", c], held["neg_mean", c] = y, neg_mean
+            nc.vector.tensor_scalar(out=neg_mean[:], in0=held["y_sum", c][:], scalar1=-1.0 / C, scalar2=None, op0=MULT)
+            held["neg_mean", c] = neg_mean
 
-        def centre(c):
-            y, neg_mean = held["y", c], held["neg_mean", c]
-            sq_sum = small.tile([P, R], F32)
-            centred = work.tile([P, R * C], F32)
-            for r in range(R):
-                cols = slice(r * C, (r + 1) * C)
-                squares = work.tile([P, C], BF16)
-                nc.scalar.activation(
-                    out=squares[:],
-                    in_=y[:, cols],
-                    func=SQUARE,
-                    bias=neg_mean[:, r : r + 1],
-                    accum_out=sq_sum[:, r : r + 1],
-                )
-                nc.vector.scalar_tensor_tensor(
-                    out=centred[:, cols],
-                    in0=y[:, cols],
-                    scalar=neg_mean[:, r : r + 1],
-                    in1=gain[:],
-                    op0=ADD,
-                    op1=MULT,
-                )
-            held["sq_sum", c], held["centred", c] = sq_sum, centred
-
-        def deviation(c):
+        def root(c):
             sd = small.tile([P, R], F32)
-            nc.scalar.activation(out=sd[:], in_=held["sq_sum", c][:], func=SQRT, bias=eps[:, 0:1], scale=1.0 / C)
+            nc.scalar.activation(out=sd[:], in_=held["sq_sum", c][:], func=SQRT, bias=eps[:, 0:1], scale=1.0 / C**3)
+            held["sd", c] = sd
+
+        def invert(c):
             inv_sd = small.tile([P, R], F32)
-            nc.vector.reciprocal(out=inv_sd[:], in_=sd[:])
+            nc.vector.reciprocal(out=inv_sd[:], in_=held["sd", c][:])
             held["inv_sd", c] = inv_sd
 
-        def scale_and_store(c):
-            result = work.tile([P, R * C], F32, bufs=3)
-            for r in range(R):
-                cols = slice(r * C, (r + 1) * C)
-                nc.vector.tensor_scalar(
-                    out=result[:, cols],
-                    in0=held["centred", c][:, cols],
-                    scalar1=held["inv_sd", c][:, r : r + 1],
-                    scalar2=None,
-                    op0=MULT,
-                )
-            nc.sync.dma_start(out=out_chunks[c], in_=result[:])
+        def centre(i):
+            c, r = divmod(i, R)
+            if r == 0:
+                centred = work.tile([P, R * C], F32)
+                held["centred", c] = centred
+            nc.vector.scalar_tensor_tensor(
+                out=held["centred", c][:, r * C : (r + 1) * C],
+                in0=held["y", c][:, r * C : (r + 1) * C],
+                scalar=held["neg_mean", c][:, r : r + 1],
+                in1=gain[:],
+                op0=ADD,
+                op1=MULT,
+            )
 
-        def run(stage, c):
-            if 0 <= c < CHUNKS:
-                stage(c)
+        def scale(i):
+            c, r = divmod(i, R)
+            if r == 0:
+                result = work.tile([P, R * C], F32)
+                held["result", c] = result
+            nc.vector.tensor_scalar(
+                out=held["result", c][:, r * C : (r + 1) * C],
+                in0=held["centred", c][:, r * C : (r + 1) * C],
+                scalar1=held["inv_sd", c][:, r : r + 1],
+                scalar2=None,
+                op0=MULT,
+            )
+
+        def store(c):
+            nc.sync.dma_start(out=out_chunks[c], in_=held["result", c][:])
+
+        def run(stage, i):
+            if 0 <= i < TILES:
+                stage(i)
+
+        def run_chunk(stage, i):
+            if 0 <= i < TILES and i % R == R - 1:
+                stage(i // R)
 
         def step(i):
-            run(transpose_words, i)
-            run(sum_squares, i)
-            run(gate_products, i + 1)
-            run(centre, i - 2)
-            run(quantise_01, i)
-            run(gate_vv, i)
-            run(deviation, i - 2)
-            run(scale_and_store, i - 2)
-            run(quantise_2, i)
-            run(square_v, i + 1)
-            run(multiply, i - 1)
-            run(residual, i - 1)
-            run(square_s, i + 2)
-            run(load, i + 3)
+            run(multiply, i - 2)
+            run(transpose_words, i + 1)
+            run(sum_squares, i + 1)
 
-        step(-3)
-        step(-2)
+            run(sum_deviations, i - 3)
+            run(square_v, i + 2)
+            run(copy_s_g2, i + 1)
+            run(square_s, i + 1)
+            run_chunk(root, i - 3)
+
+            run(product_0, i)
+            run(residual, i - 2)
+            run(product_1, i)
+            run(centre, i - 4)
+            run_chunk(negate_mean, i - 2)
+            run(product_2, i)
+            run(quantise_01, i)
+            run_chunk(invert, i - 4)
+            run(scale, i - 6)
+            run(quantise_2, i)
+            run_chunk(store, i - 6)
+
+            run_chunk(load, i + R - 1 + R * AHEAD)
+
+        load(0)
         load_weights()
-        step(-1)
-        step(0)
+        load(1)
+        load_gain()
+        for c in range(2, AHEAD - 1):
+            load(c)
+        for i in range(-2, 2):
+            step(i)
         quantise_weights()
-        for i in range(1, CHUNKS + 2):
+        for i in range(2, TILES + 7):
             step(i)

@@ -22,6 +22,7 @@ KS = PASSES * C
 PACK = 4
 HALVES = 2
 WORDS = C // 2
+RUN = 4
 R = 2
 CHUNKS = POINTS // (P * R)
 TILES = CHUNKS * R
@@ -97,7 +98,13 @@ def tile_selfinteraction_pc_t_kernel(tc, s, v, g_s, w0, ln_g0, out):
         def square_v(i):
             c, r = divmod(i, R)
             v_sq = work.tile([P, C * XYZ], F32)
-            nc.scalar.activation(out=v_sq[:], in_=held["v", c][:, r * C * XYZ : (r + 1) * C * XYZ], func=SQUARE)
+            nc.scalar.activation(
+                out=v_sq[:].rearrange("n (x b l) -> n b x l", x=PACK * XYZ, l=RUN),
+                in_=held["v", c][:, r * C * XYZ : (r + 1) * C * XYZ].rearrange(
+                    "n (b l x) -> n b x l", l=RUN, x=PACK * XYZ
+                ),
+                func=SQUARE,
+            )
             held["v_sq", i] = v_sq
 
         def transpose_words(i):
@@ -120,7 +127,7 @@ def tile_selfinteraction_pc_t_kernel(tc, s, v, g_s, w0, ln_g0, out):
             held["s_g2_bank", i], held["g01_bank", i] = s_g2_bank, g01_bank
 
         def sum_squares(i):
-            planes = held["v_sq", i][:].rearrange("n (q t j) -> n t j q", t=PACK, j=XYZ)
+            planes = held["v_sq", i][:].rearrange("n (t j q) -> n t j q", t=PACK, j=XYZ)
             vv_bank = psum.tile([P, PACK * P], F32)
             for t in range(PACK):
                 for j in range(XYZ):

@@ -26,6 +26,7 @@ RUN = 4
 R = 2
 CHUNKS = POINTS // (P * R)
 TILES = CHUNKS * R
+LAG = 3
 AHEAD = 4
 EPS = 1e-6
 
@@ -53,7 +54,11 @@ def tile_selfinteraction_pc_t_kernel(tc, s, v, g_s, w0, ln_g0, out):
         nc.vector.memset(eps[:], EPS)
         w_rows = keep.tile([P, PASSES * PACK * C], BF16)
         w_grouped = keep.tile([P, PASSES * C * PACK], BF16, align_bytes=64)
-        gain = keep.tile([P, C], BF16)
+        ones = keep.tile([P, P], BF16)
+        nc.vector.memset(ones[:], 1.0)
+        gain_row = keep.tile([P, C], BF16)
+        nc.vector.memset(gain_row[:], 0.0)
+        gain = psum.tile([P, C], F32, bufs=1)
         w_codes = keep.tile([P, PASSES * C], U32, align_bytes=64)
         w_scales = keep.tile([P, PASSES * C], U8, align_bytes=64)
 
@@ -64,7 +69,8 @@ def tile_selfinteraction_pc_t_kernel(tc, s, v, g_s, w0, ln_g0, out):
             )
 
         def load_gain():
-            nc.sync.dma_start(out=gain[:], in_=ln_g0.partition_broadcast(P))
+            nc.sync.dma_start(out=gain_row[:1, :], in_=ln_g0.rearrange("(o c) -> o c", o=1))
+            nc.tensor.matmul(gain[:], lhsT=ones[:], rhs=gain_row[:], start=True, stop=True)
 
         def quantise_weights():
             def grouped(g):
@@ -73,7 +79,7 @@ def tile_selfinteraction_pc_t_kernel(tc, s, v, g_s, w0, ln_g0, out):
             def rows(g):
                 return w_rows[:, g * PACK * C : (g + 1) * PACK * C].rearrange("p (t c) -> p c t", t=PACK)
 
-            nc.gpsimd.tensor_scalar(out=grouped(2), in0=rows(2), scalar1=1.0, scalar2=0.0, op0=MULT, op1=ADD)
+            nc.scalar.copy(out=grouped(2), in_=rows(2))
             for g in range(2):
                 nc.vector.tensor_copy(out=grouped(g), in_=rows(g))
             for g in range(PASSES):
@@ -87,7 +93,7 @@ def tile_selfinteraction_pc_t_kernel(tc, s, v, g_s, w0, ln_g0, out):
             v_t = loads.tile([P, R * C * XYZ], BF16)
             s_t = loads.tile([P, R * C], BF16)
             g_t = loads.tile([P, R * KS], BF16)
-            parts = R if c == 0 else 1
+            parts = R if c < 2 else 1
             for part in range(parts):
                 for held_tile, rows in ((v_t, v_chunks[c]), (s_t, s_chunks[c]), (g_t, g_chunks[c])):
                     width = rows.shape[1] // parts
@@ -107,24 +113,25 @@ def tile_selfinteraction_pc_t_kernel(tc, s, v, g_s, w0, ln_g0, out):
             )
             held["v_sq", i] = v_sq
 
-        def transpose_words(i):
+        def transpose_words(bank, b, words, first):
+            for h in range(HALVES):
+                nc.tensor.transpose(
+                    bank[:, (b + h) * P : (b + h + 1) * P], words[:, first + h : first + WORDS : HALVES], ident[:]
+                )
+
+        def transpose_s_g2(i):
             c, r = divmod(i, R)
-            s_words = held["s", c][:, r * C : (r + 1) * C].bitcast(F32)
-            g_words = held["g", c][:, r * KS : (r + 1) * KS].bitcast(F32)
             s_g2_bank = psum.tile([P, 2 * WORDS], F32)
+            transpose_words(s_g2_bank, 0, held["s", c][:].bitcast(F32), r * WORDS)
+            transpose_words(s_g2_bank, HALVES, held["g", c][:].bitcast(F32), (r * PASSES + 2) * WORDS)
+            held["s_g2_bank", i] = s_g2_bank
+
+        def transpose_g01(i):
+            c, r = divmod(i, R)
             g01_bank = psum.tile([P, 2 * WORDS], F32)
-            for bank, place, words, first in (
-                (s_g2_bank, 0, s_words, 0),
-                (s_g2_bank, 1, g_words, 2 * WORDS),
-                (g01_bank, 0, g_words, 0),
-                (g01_bank, 1, g_words, WORDS),
-            ):
-                for h in range(HALVES):
-                    b = place * HALVES + h
-                    nc.tensor.transpose(
-                        bank[:, b * P : (b + 1) * P], words[:, first + h : first + WORDS : HALVES], ident[:]
-                    )
-            held["s_g2_bank", i], held["g01_bank", i] = s_g2_bank, g01_bank
+            for g in range(2):
+                transpose_words(g01_bank, g * HALVES, held["g", c][:].bitcast(F32), (r * PASSES + g) * WORDS)
+            held["g01_bank", i] = g01_bank
 
         def sum_squares(i):
             planes = held["v_sq", i][:].rearrange("n (t j q) -> n t j q", t=PACK, j=XYZ)
@@ -152,7 +159,7 @@ def tile_selfinteraction_pc_t_kernel(tc, s, v, g_s, w0, ln_g0, out):
 
         def square_s(i):
             ss_t = work.tile([P, C], F32)
-            nc.scalar.activation(out=ss_t[:], in_=held["s_t", i], func=SQUARE)
+            nc.gpsimd.tensor_tensor(out=ss_t[:], in0=held["s_t", i], in1=held["s_t", i], op=MULT)
             held["ss_t", i] = ss_t
 
         def product(i, g, factor):
@@ -183,8 +190,8 @@ def tile_selfinteraction_pc_t_kernel(tc, s, v, g_s, w0, ln_g0, out):
             )
 
         def quantise_01(i):
-            codes = work.tile([P, PASSES * P], U32, align_bytes=64)
-            scales = work.tile([P, PASSES * P], U8, align_bytes=64)
+            codes = work.tile([P, PASSES * P], U32, align_bytes=64, bufs=LAG + 2)
+            scales = work.tile([P, PASSES * P], U8, align_bytes=64, bufs=LAG + 2)
             held["codes", i], held["scales", i] = codes, scales
             nc.vector.quantize_mx(
                 out=codes[:, : 2 * P].bitcast(FP8X4), scales=scales[:, : 2 * P], in_=held["u", i][:, : 2 * C]
@@ -198,7 +205,7 @@ def tile_selfinteraction_pc_t_kernel(tc, s, v, g_s, w0, ln_g0, out):
             )
 
         def multiply(i):
-            acc = psum.tile([P, C], F32)
+            acc = psum.tile([P, C], F32, bufs=1)
             for g in range(PASSES):
                 nc.tensor.matmul_mx(
                     out=acc[:],
@@ -276,12 +283,13 @@ def tile_selfinteraction_pc_t_kernel(tc, s, v, g_s, w0, ln_g0, out):
             if r == 0:
                 result = work.tile([P, R * C], F32)
                 held["result", c] = result
-            nc.vector.tensor_scalar(
+            nc.gpsimd.tensor_scalar(
                 out=held["result", c][:, r * C : (r + 1) * C],
                 in0=held["centred", c][:, r * C : (r + 1) * C],
                 scalar1=held["inv_sd", c][:, r : r + 1],
-                scalar2=None,
+                scalar2=0.0,
                 op0=MULT,
+                op1=ADD,
             )
 
         def store(c):
@@ -296,38 +304,38 @@ def tile_selfinteraction_pc_t_kernel(tc, s, v, g_s, w0, ln_g0, out):
                 stage(i // R)
 
         def step(i):
-            run(multiply, i - 2)
-            run(transpose_words, i + 1)
+            run(multiply, i - LAG)
+            run(transpose_g01, i + 1)
             run(sum_squares, i + 1)
+            run(transpose_s_g2, i + 2)
 
-            run(sum_deviations, i - 3)
-            run(square_v, i + 2)
             run(copy_s_g2, i + 1)
+            run(sum_deviations, i - LAG - 1)
+            run(square_v, i + 2)
+            run_chunk(root, i - LAG - 1)
             run(square_s, i + 1)
-            run_chunk(root, i - 3)
+            run(scale, i - LAG - 4)
 
             run(product_0, i)
-            run(residual, i - 2)
             run(product_1, i)
-            run(centre, i - 4)
-            run_chunk(negate_mean, i - 2)
+            run(centre, i - LAG - 2)
+            run_chunk(invert, i - LAG - 2)
             run(product_2, i)
+            run(residual, i - LAG)
             run(quantise_01, i)
-            run_chunk(invert, i - 4)
-            run(scale, i - 6)
+            run_chunk(negate_mean, i - LAG)
             run(quantise_2, i)
-            run_chunk(store, i - 6)
+            run_chunk(store, i - LAG - 4)
 
             run_chunk(load, i + R - 1 + R * AHEAD)
 
         load(0)
         load_weights()
-        load(1)
         load_gain()
-        for c in range(2, AHEAD - 1):
+        for c in range(1, AHEAD - 1):
             load(c)
         for i in range(-2, 2):
             step(i)
         quantise_weights()
-        for i in range(2, TILES + 7):
+        for i in range(2, TILES + LAG + 5):
             step(i)

@@ -52,6 +52,8 @@ def tile_selfinteraction_pc_t_kernel(tc, s, v, g_s, w0, ln_g0, out):
         make_identity(nc, ident[:])
         eps = keep.tile([P, 1], F32)
         nc.vector.memset(eps[:], EPS)
+        warm = keep.tile([P, 1], F32)
+        nc.scalar.activation(out=warm[:], in_=eps[:], func=SQRT)
         w_rows = keep.tile([P, PASSES * PACK * C], BF16)
         w_grouped = keep.tile([P, PASSES * C * PACK], BF16, align_bytes=64)
         ones = keep.tile([P, P], BF16)
@@ -70,6 +72,8 @@ def tile_selfinteraction_pc_t_kernel(tc, s, v, g_s, w0, ln_g0, out):
 
         def load_gain():
             nc.sync.dma_start(out=gain_row[:1, :], in_=ln_g0.rearrange("(o c) -> o c", o=1))
+
+        def spread_gain():
             nc.tensor.matmul(gain[:], lhsT=ones[:], rhs=gain_row[:], start=True, stop=True)
 
         def quantise_weights():
@@ -336,6 +340,7 @@ def tile_selfinteraction_pc_t_kernel(tc, s, v, g_s, w0, ln_g0, out):
             load(c)
         for i in range(-2, 2):
             step(i)
+        spread_gain()
         quantise_weights()
         for i in range(2, TILES + LAG + 5):
             step(i)

@@ -11,7 +11,7 @@ FP8X4 = mybir.dt.float8_e4m3fn_x4
 MULT = mybir.AluOpType.mult
 ADD = mybir.AluOpType.add
 SQUARE = mybir.ActivationFunctionType.Square
-SQRT = mybir.ActivationFunctionType.Sqrt
+RECIPROCAL_SQRT = mybir.ActivationFunctionType.Abs_reciprocal_sqrt
 
 P = 128
 POINTS = 4096
@@ -26,7 +26,7 @@ RUN = 4
 R = 2
 CHUNKS = POINTS // (P * R)
 TILES = CHUNKS * R
-LAG = 3
+LAG = 2
 AHEAD = 4
 EPS = 1e-6
 
@@ -53,7 +53,7 @@ def tile_selfinteraction_pc_t_kernel(tc, s, v, g_s, w0, ln_g0, out):
         eps = keep.tile([P, 1], F32)
         nc.vector.memset(eps[:], EPS)
         warm = keep.tile([P, 1], F32)
-        nc.scalar.activation(out=warm[:], in_=eps[:], func=SQRT)
+        nc.scalar.activation(out=warm[:], in_=eps[:], func=RECIPROCAL_SQRT)
         w_rows = keep.tile([P, PASSES * PACK * C], BF16)
         w_grouped = keep.tile([P, PASSES * C * PACK], BF16, align_bytes=64)
         ones = keep.tile([P, P], BF16)
@@ -64,11 +64,10 @@ def tile_selfinteraction_pc_t_kernel(tc, s, v, g_s, w0, ln_g0, out):
         w_codes = keep.tile([P, PASSES * C], U32, align_bytes=64)
         w_scales = keep.tile([P, PASSES * C], U8, align_bytes=64)
 
-        def load_weights():
-            nc.sync.dma_start(
-                out=w_rows[:].rearrange("p (g x) -> p g x", g=PASSES),
-                in_=w0.rearrange("(g p t) c -> p g (t c)", g=PASSES, p=P, t=PACK),
-            )
+        w_passes = w0.rearrange("(g p t) c -> g p (t c)", g=PASSES, p=P, t=PACK)
+
+        def load_weights(g):
+            nc.sync.dma_start(out=w_rows[:, g * PACK * C : (g + 1) * PACK * C], in_=w_passes[g])
 
         def load_gain():
             nc.sync.dma_start(out=gain_row[:1, :], in_=ln_g0.rearrange("(o c) -> o c", o=1))
@@ -76,34 +75,35 @@ def tile_selfinteraction_pc_t_kernel(tc, s, v, g_s, w0, ln_g0, out):
         def spread_gain():
             nc.tensor.matmul(gain[:], lhsT=ones[:], rhs=gain_row[:], start=True, stop=True)
 
-        def quantise_weights():
-            def grouped(g):
-                return w_grouped[:, g * C * PACK : (g + 1) * C * PACK].rearrange("p (c t) -> p c t", t=PACK)
+        def regroup_weights(g):
+            cols = slice(g * C * PACK, (g + 1) * C * PACK)
+            nc.vector.tensor_copy(
+                out=w_grouped[:, cols].rearrange("p (c t) -> p c t", t=PACK),
+                in_=w_rows[:, cols].rearrange("p (t c) -> p c t", t=PACK),
+            )
 
-            def rows(g):
-                return w_rows[:, g * PACK * C : (g + 1) * PACK * C].rearrange("p (t c) -> p c t", t=PACK)
+        def quantise_weights(g):
+            nc.vector.quantize_mx(
+                out=w_codes[:, g * C : (g + 1) * C].bitcast(FP8X4),
+                scales=w_scales[:, g * C : (g + 1) * C],
+                in_=w_grouped[:, g * C * PACK : (g + 1) * C * PACK],
+            )
 
-            nc.scalar.copy(out=grouped(2), in_=rows(2))
-            for g in range(2):
-                nc.vector.tensor_copy(out=grouped(g), in_=rows(g))
-            for g in range(PASSES):
-                nc.vector.quantize_mx(
-                    out=w_codes[:, g * C : (g + 1) * C].bitcast(FP8X4),
-                    scales=w_scales[:, g * C : (g + 1) * C],
-                    in_=w_grouped[:, g * C * PACK : (g + 1) * C * PACK],
-                )
-
-        def load(c):
+        def make_room(c):
             v_t = loads.tile([P, R * C * XYZ], BF16)
             s_t = loads.tile([P, R * C], BF16)
             g_t = loads.tile([P, R * KS], BF16)
-            parts = R if c < 2 else 1
-            for part in range(parts):
-                for held_tile, rows in ((v_t, v_chunks[c]), (s_t, s_chunks[c]), (g_t, g_chunks[c])):
-                    width = rows.shape[1] // parts
-                    cols = slice(part * width, (part + 1) * width)
-                    nc.sync.dma_start(out=held_tile[:, cols], in_=rows[:, cols])
             held["s", c], held["v", c], held["g", c] = s_t, v_t, g_t
+
+        def load_part(c, first, last):
+            for name, rows in (("v", v_chunks[c]), ("s", s_chunks[c]), ("g", g_chunks[c])):
+                width = rows.shape[1] // R
+                cols = slice(first * width, last * width)
+                nc.sync.dma_start(out=held[name, c][:, cols], in_=rows[:, cols])
+
+        def load(c):
+            make_room(c)
+            load_part(c, 0, R)
 
         def square_v(i):
             c, r = divmod(i, R)
@@ -132,7 +132,7 @@ def tile_selfinteraction_pc_t_kernel(tc, s, v, g_s, w0, ln_g0, out):
 
         def transpose_g01(i):
             c, r = divmod(i, R)
-            g01_bank = psum.tile([P, 2 * WORDS], F32)
+            g01_bank = psum.tile([P, 2 * WORDS], F32, name="g01_bank")
             for g in range(2):
                 transpose_words(g01_bank, g * HALVES, held["g", c][:].bitcast(F32), (r * PASSES + g) * WORDS)
             held["g01_bank", i] = g01_bank
@@ -163,7 +163,10 @@ def tile_selfinteraction_pc_t_kernel(tc, s, v, g_s, w0, ln_g0, out):
 
         def square_s(i):
             ss_t = work.tile([P, C], F32)
-            nc.gpsimd.tensor_tensor(out=ss_t[:], in0=held["s_t", i], in1=held["s_t", i], op=MULT)
+            if i < 2:
+                nc.scalar.activation(out=ss_t[:], in_=held["s_t", i], func=SQUARE)
+            else:
+                nc.gpsimd.tensor_tensor(out=ss_t[:], in0=held["s_t", i], in1=held["s_t", i], op=MULT)
             held["ss_t", i] = ss_t
 
         def product(i, g, factor):
@@ -209,7 +212,10 @@ def tile_selfinteraction_pc_t_kernel(tc, s, v, g_s, w0, ln_g0, out):
             )
 
         def multiply(i):
-            acc = psum.tile([P, C], F32, bufs=1)
+            if i < TILES - LAG:
+                acc = psum.tile([P, C], F32, bufs=1)
+            else:
+                acc = psum.tile([P, C], F32, name="g01_bank")
             for g in range(PASSES):
                 nc.tensor.matmul_mx(
                     out=acc[:],
@@ -255,17 +261,16 @@ def tile_selfinteraction_pc_t_kernel(tc, s, v, g_s, w0, ln_g0, out):
 
         def negate_mean(c):
             neg_mean = small.tile([P, R], F32)
-            nc.vector.tensor_scalar(out=neg_mean[:], in0=held["y_sum", c][:], scalar1=-1.0 / C, scalar2=None, op0=MULT)
+            nc.gpsimd.tensor_scalar(
+                out=neg_mean[:], in0=held["y_sum", c][:], scalar1=-1.0 / C, scalar2=0.0, op0=MULT, op1=ADD
+            )
             held["neg_mean", c] = neg_mean
 
-        def root(c):
-            sd = small.tile([P, R], F32)
-            nc.scalar.activation(out=sd[:], in_=held["sq_sum", c][:], func=SQRT, bias=eps[:, 0:1], scale=1.0 / C**3)
-            held["sd", c] = sd
-
-        def invert(c):
+        def invert_sd(c):
             inv_sd = small.tile([P, R], F32)
-            nc.vector.reciprocal(out=inv_sd[:], in_=held["sd", c][:])
+            nc.scalar.activation(
+                out=inv_sd[:], in_=held["sq_sum", c][:], func=RECIPROCAL_SQRT, bias=eps[:, 0:1], scale=1.0 / C**3
+            )
             held["inv_sd", c] = inv_sd
 
         def centre(i):
@@ -287,7 +292,8 @@ def tile_selfinteraction_pc_t_kernel(tc, s, v, g_s, w0, ln_g0, out):
             if r == 0:
                 result = work.tile([P, R * C], F32)
                 held["result", c] = result
-            nc.gpsimd.tensor_scalar(
+            engine = nc.gpsimd if c < CHUNKS - 1 else nc.vector
+            engine.tensor_scalar(
                 out=held["result", c][:, r * C : (r + 1) * C],
                 in0=held["centred", c][:, r * C : (r + 1) * C],
                 scalar1=held["inv_sd", c][:, r : r + 1],
@@ -314,33 +320,43 @@ def tile_selfinteraction_pc_t_kernel(tc, s, v, g_s, w0, ln_g0, out):
             run(transpose_s_g2, i + 2)
 
             run(copy_s_g2, i + 1)
+            run(square_s, i + 1)
             run(sum_deviations, i - LAG - 1)
             run(square_v, i + 2)
-            run_chunk(root, i - LAG - 1)
-            run(square_s, i + 1)
-            run(scale, i - LAG - 4)
+            run_chunk(invert_sd, i - LAG - 1)
+            run(scale, i - LAG - 3)
 
             run(product_0, i)
             run(product_1, i)
             run(centre, i - LAG - 2)
-            run_chunk(invert, i - LAG - 2)
             run(product_2, i)
             run(residual, i - LAG)
-            run(quantise_01, i)
             run_chunk(negate_mean, i - LAG)
+            run(quantise_01, i)
             run(quantise_2, i)
-            run_chunk(store, i - LAG - 4)
+            run_chunk(store, i - LAG - 3)
 
             run_chunk(load, i + R - 1 + R * AHEAD)
 
-        load(0)
-        load_weights()
+        make_room(0)
+        for r in range(R):
+            load_weights(r)
+            load_part(0, r, r + 1)
+        load_weights(R)
+        make_room(1)
+        for r in range(R):
+            load_part(1, r, r + 1)
         load_gain()
-        for c in range(1, AHEAD - 1):
-            load(c)
-        for i in range(-2, 2):
+        load(2)
+        regroup_weights(0)
+        quantise_weights(0)
+        regroup_weights(1)
+        for i in range(-2, 1):
             step(i)
+        quantise_weights(1)
+        regroup_weights(2)
+        step(1)
+        quantise_weights(2)
         spread_gain()
-        quantise_weights()
-        for i in range(2, TILES + LAG + 5):
+        for i in range(2, TILES + LAG + 4):
             step(i)

@@ -302,8 +302,13 @@ def tile_selfinteraction_pc_t_kernel(tc, s, v, g_s, w0, ln_g0, out):
                 op1=ADD,
             )
 
-        def store(c):
-            nc.sync.dma_start(out=out_chunks[c], in_=held["result", c][:])
+        def store(i):
+            c, r = divmod(i, R)
+            if c == CHUNKS - 1:
+                cols = slice(r * C, (r + 1) * C)
+                nc.sync.dma_start(out=out_chunks[c][:, cols], in_=held["result", c][:, cols])
+            elif r == R - 1:
+                nc.sync.dma_start(out=out_chunks[c], in_=held["result", c][:])
 
         def run(stage, i):
             if 0 <= i < TILES:
@@ -325,16 +330,16 @@ def tile_selfinteraction_pc_t_kernel(tc, s, v, g_s, w0, ln_g0, out):
             run(square_v, i + 2)
             run_chunk(invert_sd, i - LAG - 1)
             run(scale, i - LAG - 3)
+            run(store, i - LAG - 3)
 
             run(product_0, i)
             run(product_1, i)
-            run(centre, i - LAG - 2)
-            run(product_2, i)
             run(residual, i - LAG)
+            run(product_2, i)
             run_chunk(negate_mean, i - LAG)
             run(quantise_01, i)
+            run(centre, i - LAG - 2)
             run(quantise_2, i)
-            run_chunk(store, i - LAG - 3)
 
             run_chunk(load, i + R - 1 + R * AHEAD)
 

import math

import concourse.mybir as mybir
from concourse.masks import make_identity

F32 = mybir.dt.float32
BF16 = mybir.dt.bfloat16
U32 = mybir.dt.uint32
U8 = mybir.dt.uint8
FP8X4 = mybir.dt.float8_e4m3fn_x4
MULT = mybir.AluOpType.mult
ADD = mybir.AluOpType.add
SQUARE = mybir.ActivationFunctionType.Square
RECIPROCAL_SQRT = mybir.ActivationFunctionType.Abs_reciprocal_sqrt

P = 128
POINTS = 4096
C = 512
XYZ = 3
PASSES = 3
KS = PASSES * C
PACK = 4
HALVES = 2
WORDS = C // 2
RUN = 4
R = 2
CHUNKS = POINTS // (P * R)
TILES = CHUNKS * R
LAG = 2
AHEAD = 4
EPS = 1e-6

FLOPS = 2 * POINTS * KS * C


def tile_selfinteraction_pc_t_kernel(tc, s, v, g_s, w0, ln_g0, out):
    nc = tc.nc

    s_chunks = s.rearrange("(k p r) c -> k p (r c)", p=P, r=R)
    g_chunks = g_s.rearrange("(k p r) c -> k p (r c)", p=P, r=R)
    v_chunks = v.rearrange("(k p r) c j -> k p (r c j)", p=P, r=R)
    out_chunks = out.rearrange("(k p r) c -> k p (r c)", p=P, r=R)

    with tc.tile_pool(name="keep", bufs=1) as keep, tc.tile_pool(name="loads", bufs=AHEAD + 2) as loads, tc.tile_pool(
        name="work", bufs=3
    ) as work, tc.tile_pool(name="small", bufs=4) as small, tc.psum_pool(
        name="psum", bufs=2
    ) as psum, tc.manual_schedule():
        held = {}

        ident = keep.tile([P, P], F32)
        make_identity(nc, ident[:])
        eps = keep.tile([P, 1], F32)
        nc.vector.memset(eps[:], EPS)
        warm = keep.tile([P, 1], F32)
        nc.scalar.activation(out=warm[:], in_=eps[:], func=RECIPROCAL_SQRT)
        w_rows = keep.tile([P, PASSES * PACK * C], BF16)
        w_grouped = keep.tile([P, PASSES * C * PACK], BF16, align_bytes=64)
        ones = keep.tile([P, P], BF16)
        nc.vector.memset(ones[:], 1.0)
        gain_row = keep.tile([P, C], BF16)
        nc.vector.memset(gain_row[:], 0.0)
        gain = psum.tile([P, C], F32, bufs=1)
        w_codes = keep.tile([P, PASSES * C], U32, align_bytes=64)
        w_scales = keep.tile([P, PASSES * C], U8, align_bytes=64)

        w_passes = w0.rearrange("(g p t) c -> g p (t c)", g=PASSES, p=P, t=PACK)

        def load_weights(g):
            nc.sync.dma_start(out=w_rows[:, g * PACK * C : (g + 1) * PACK * C], in_=w_passes[g])

        def load_gain():
            nc.sync.dma_start(out=gain_row[:1, :], in_=ln_g0.rearrange("(o c) -> o c", o=1))

        def spread_gain():
            nc.tensor.matmul(gain[:], lhsT=ones[:], rhs=gain_row[:], start=True, stop=True)

        def regroup_weights(g):
            cols = slice(g * C * PACK, (g + 1) * C * PACK)
            nc.vector.tensor_copy(
                out=w_grouped[:, cols].rearrange("p (c t) -> p c t", t=PACK),
                in_=w_rows[:, cols].rearrange("p (t c) -> p c t", t=PACK),
            )

        def quantise_weights(g):
            nc.vector.quantize_mx(
                out=w_codes[:, g * C : (g + 1) * C].bitcast(FP8X4),
                scales=w_scales[:, g * C : (g + 1) * C],
                in_=w_grouped[:, g * C * PACK : (g + 1) * C * PACK],
            )

        def make_room(c):
            v_t = loads.tile([P, R * C * XYZ], BF16)
            s_t = loads.tile([P, R * C], BF16)
            g_t = loads.tile([P, R * KS], BF16)
            held["s", c], held["v", c], held["g", c] = s_t, v_t, g_t

        def load_part(c, first, last):
            for name, rows in (("v", v_chunks[c]), ("s", s_chunks[c]), ("g", g_chunks[c])):
                width = rows.shape[1] // R
                cols = slice(first * width, last * width)
                nc.sync.dma_start(out=held[name, c][:, cols], in_=rows[:, cols])

        def load(c):
            make_room(c)
            load_part(c, 0, R)

        def square_v(i):
            c, r = divmod(i, R)
            v_sq = work.tile([P, C * XYZ], F32)
            nc.scalar.activation(
                out=v_sq[:].rearrange("n (x b l) -> n b x l", x=PACK * XYZ, l=RUN),
                in_=held["v", c][:, r * C * XYZ : (r + 1) * C * XYZ].rearrange(
                    "n (b l x) -> n b x l", l=RUN, x=PACK * XYZ
                ),
                func=SQUARE,
            )
            held["v_sq", i] = v_sq

        def transpose_words(bank, b, words, first):
            for h in range(HALVES):
                nc.tensor.transpose(
                    bank[:, (b + h) * P : (b + h + 1) * P], words[:, first + h : first + WORDS : HALVES], ident[:]
                )

        def transpose_s_g2(i):
            c, r = divmod(i, R)
            s_g2_bank = psum.tile([P, 2 * WORDS], F32)
            transpose_words(s_g2_bank, 0, held["s", c][:].bitcast(F32), r * WORDS)
            transpose_words(s_g2_bank, HALVES, held["g", c][:].bitcast(F32), (r * PASSES + 2) * WORDS)
            held["s_g2_bank", i] = s_g2_bank

        def transpose_g01(i):
            c, r = divmod(i, R)
            g01_bank = psum.tile([P, 2 * WORDS], F32, name="g01_bank")
            for g in range(2):
                transpose_words(g01_bank, g * HALVES, held["g", c][:].bitcast(F32), (r * PASSES + g) * WORDS)
            held["g01_bank", i] = g01_bank

        def sum_squares(i):
            planes = held["v_sq", i][:].rearrange("n (t j q) -> n t j q", t=PACK, j=XYZ)
            vv_bank = psum.tile([P, PACK * P], F32)
            for t in range(PACK):
                for j in range(XYZ):
                    nc.tensor.matmul(
                        vv_bank[:, t * P : (t + 1) * P],
                        lhsT=planes[:, t, j, :],
                        rhs=ident[:],
                        is_transpose=True,
                        start=(j == 0),
                        stop=(j == XYZ - 1),
                    )
            held["vv_bank", i] = vv_bank

        def copy_s_g2(i):
            s_g2 = work.tile([P, 2 * WORDS], F32)
            nc.scalar.copy(
                out=s_g2[:].rearrange("p (x n h) -> p x n h", x=2, h=HALVES),
                in_=held["s_g2_bank", i][:].rearrange("p (x h n) -> p x n h", x=2, h=HALVES),
            )
            held["s_t", i] = s_g2[:, :WORDS].bitcast(BF16)
            held["g2_t", i] = s_g2[:, WORDS:].bitcast(BF16)

        def square_s(i):
            ss_t = work.tile([P, C], F32)
            if i < 2:
                nc.scalar.activation(out=ss_t[:], in_=held["s_t", i], func=SQUARE)
            else:
                nc.gpsimd.tensor_tensor(out=ss_t[:], in0=held["s_t", i], in1=held["s_t", i], op=MULT)
            held["ss_t", i] = ss_t

        def product(i, g, factor):
            gate = held["g01_bank", i][:, g * WORDS : (g + 1) * WORDS].bitcast(BF16)
            nc.vector.tensor_tensor(
                out=held["u", i][:, g * C : (g + 1) * C].rearrange("p (n h e) -> p n h e", h=HALVES, e=2),
                in0=gate.rearrange("p (h n e) -> p n h e", h=HALVES, e=2),
                in1=factor.rearrange("p (n h e) -> p n h e", h=HALVES, e=2),
                op=MULT,
            )

        def product_0(i):
            u = work.tile([P, KS], BF16, align_bytes=64)
            held["u", i] = u
            product(i, 0, held["s_t", i])

        def product_1(i):
            product(i, 1, held["ss_t", i][:])

        def product_2(i):
            nc.vector.scalar_tensor_tensor(
                out=held["u", i][:, 2 * C :].rearrange("p (n t) -> p n t", t=PACK),
                in0=held["vv_bank", i][:].rearrange("p (t n) -> p n t", t=PACK),
                scalar=1.0 / math.sqrt(3.0),
                in1=held["g2_t", i].rearrange("p (n t) -> p n t", t=PACK),
                op0=MULT,
                op1=MULT,
            )

        def quantise_01(i):
            codes = work.tile([P, PASSES * P], U32, align_bytes=64, bufs=LAG + 2)
            scales = work.tile([P, PASSES * P], U8, align_bytes=64, bufs=LAG + 2)
            held["codes", i], held["scales", i] = codes, scales
            nc.vector.quantize_mx(
                out=codes[:, : 2 * P].bitcast(FP8X4), scales=scales[:, : 2 * P], in_=held["u", i][:, : 2 * C]
            )

        def quantise_2(i):
            nc.vector.quantize_mx(
                out=held["codes", i][:, 2 * P :].bitcast(FP8X4),
                scales=held["scales", i][:, 2 * P :],
                in_=held["u", i][:, 2 * C :],
            )

        def multiply(i):
            if i < TILES - LAG:
                acc = psum.tile([P, C], F32, bufs=1)
            else:
                acc = psum.tile([P, C], F32, name="g01_bank")
            for g in range(PASSES):
                nc.tensor.matmul_mx(
                    out=acc[:],
                    lhsT=held["codes", i][:, g * P : (g + 1) * P].bitcast(FP8X4),
                    lhsT_scale=held["scales", i][:, g * P : (g + 1) * P],
                    rhs=w_codes[:, g * C : (g + 1) * C].bitcast(FP8X4),
                    rhs_scale=w_scales[:, g * C : (g + 1) * C],
                    start=(g == 0),
                    stop=(g == PASSES - 1),
                )
            held["acc", i] = acc

        def residual(i):
            c, r = divmod(i, R)
            if r == 0:
                y = work.tile([P, R * C], F32, bufs=4)
                y_sum = small.tile([P, R], F32)
                held["y", c], held["y_sum", c] = y, y_sum
            nc.vector.scalar_tensor_tensor(
                out=held["y", c][:, r * C : (r + 1) * C],
                in0=held["acc", i][:],
                scalar=1.0 / math.sqrt(KS),
                in1=held["s", c][:, r * C : (r + 1) * C],
                op0=MULT,
                op1=ADD,
                accum_out=held["y_sum", c][:, r : r + 1],
            )

        def sum_deviations(i):
            c, r = divmod(i, R)
            if r == 0:
                sq_sum = small.tile([P, R], F32)
                held["sq_sum", c] = sq_sum
            squares = work.tile([P, C], BF16)
            nc.scalar.activation(
                out=squares[:],
                in_=held["y", c][:, r * C : (r + 1) * C],
                func=SQUARE,
                bias=held["y_sum", c][:, r : r + 1],
                scale=-float(C),
                accum_out=held["sq_sum", c][:, r : r + 1],
            )

        def negate_mean(c):
            neg_mean = small.tile([P, R], F32)
            nc.gpsimd.tensor_scalar(
                out=neg_mean[:], in0=held["y_sum", c][:], scalar1=-1.0 / C, scalar2=0.0, op0=MULT, op1=ADD
            )
            held["neg_mean", c] = neg_mean

        def invert_sd(c):
            inv_sd = small.tile([P, R], F32)
            nc.scalar.activation(
                out=inv_sd[:], in_=held["sq_sum", c][:], func=RECIPROCAL_SQRT, bias=eps[:, 0:1], scale=1.0 / C**3
            )
            held["inv_sd", c] = inv_sd

        def centre(i):
            c, r = divmod(i, R)
            if r == 0:
                centred = work.tile([P, R * C], F32)
                held["centred", c] = centred
            nc.vector.scalar_tensor_tensor(
                out=held["centred", c][:, r * C : (r + 1) * C],
                in0=held["y", c][:, r * C : (r + 1) * C],
                scalar=held["neg_mean", c][:, r : r + 1],
                in1=gain[:],
                op0=ADD,
                op1=MULT,
            )

        def scale(i):
            c, r = divmod(i, R)
            if r == 0:
                result = work.tile([P, R * C], F32)
                held["result", c] = result
            engine = nc.gpsimd if c < CHUNKS - 1 else nc.vector
            engine.tensor_scalar(
                out=held["result", c][:, r * C : (r + 1) * C],
                in0=held["centred", c][:, r * C : (r + 1) * C],
                scalar1=held["inv_sd", c][:, r : r + 1],
                scalar2=0.0,
                op0=MULT,
                op1=ADD,
            )

        def store(i):
            c, r = divmod(i, R)
            if c == CHUNKS - 1:
                cols = slice(r * C, (r + 1) * C)
                nc.sync.dma_start(out=out_chunks[c][:, cols], in_=held["result", c][:, cols])
            elif r == R - 1:
                nc.sync.dma_start(out=out_chunks[c], in_=held["result", c][:])

        def run(stage, i):
            if 0 <= i < TILES:
                stage(i)

        def run_chunk(stage, i):
            if 0 <= i < TILES and i % R == R - 1:
                stage(i // R)

        def step(i):
            run(multiply, i - LAG)
            run(transpose_g01, i + 1)
            run(sum_squares, i + 1)
            run(transpose_s_g2, i + 2)

            run(copy_s_g2, i + 1)
            run(square_s, i + 1)
            run(sum_deviations, i - LAG - 1)
            run(square_v, i + 2)
            run_chunk(invert_sd, i - LAG - 1)
            run(scale, i - LAG - 3)
            run(store, i - LAG - 3)

            run(product_0, i)
            run(product_1, i)
            run(residual, i - LAG)
            run(product_2, i)
            run_chunk(negate_mean, i - LAG)
            run(quantise_01, i)
            run(centre, i - LAG - 2)
            run(quantise_2, i)

            run_chunk(load, i + R - 1 + R * AHEAD)

        make_room(0)
        for r in range(R):
            load_weights(r)
            load_part(0, r, r + 1)
        load_weights(R)
        make_room(1)
        for r in range(R):
            load_part(1, r, r + 1)
        load_gain()
        load(2)
        regroup_weights(0)
        quantise_weights(0)
        regroup_weights(1)
        for i in range(-2, 1):
            step(i)
        quantise_weights(1)
        regroup_weights(2)
        step(1)
        quantise_weights(2)
        spread_gain()
        for i in range(2, TILES + LAG + 4):
            step(i)
